import numpy as np
import ml_dtypes


BF16 = ml_dtypes.bfloat16


def bf(x):
    return np.asarray(x, np.float32).astype(BF16)


def f64(x):
    return np.asarray(x).astype(np.float64)


E2M1 = np.array([0.0, 0.5, 1.0, 1.5, 2.0, 3.0, 4.0, 6.0, -0.0, -0.5, -1.0, -1.5, -2.0, -3.0, -4.0, -6.0])


def pack_weight(w, fmt):
    k, n = w.shape
    w = f64(bf(w)).reshape(k // 32, 32, n)
    amax = np.abs(w).max(1)
    if fmt == "e4m3":
        byte = np.frexp(amax)[1] - 1 + 127 - 7
    else:
        mant, ex = np.frexp(amax / 6.0)
        byte = np.where(mant > 0.5, ex, ex - 1) + 127
    byte = np.clip(np.where(amax > 0, byte, 1), 1, 254)
    scaled = (w * np.exp2(127.0 - byte)[:, None, :]).reshape(k, n).astype(np.float32)
    by_word = np.ascontiguousarray(scaled.reshape(k // 512, 128, 4, n).transpose(0, 1, 3, 2))
    if fmt == "e4m3":
        words = by_word.astype(ml_dtypes.float8_e4m3fn).view(np.uint8)
    else:
        c = by_word.astype(ml_dtypes.float4_e2m1fn).view(np.uint8) & 0xF
        words = c[..., 0::2] | (c[..., 1::2] << 4)
    return np.ascontiguousarray(words), np.ascontiguousarray(byte.astype(np.uint8).reshape(k // 512, 16, n))


def unpack_weight(words, scales, fmt):
    g, p, n, _ = words.shape
    if fmt == "e4m3":
        vals = np.ascontiguousarray(words).view(ml_dtypes.float8_e4m3fn).astype(np.float64)
    else:
        nib = np.empty((g, p, n, 4), np.uint8)
        nib[..., 0::2] = words & 0xF
        nib[..., 1::2] = words >> 4
        vals = E2M1[nib]
    vals = vals * np.repeat(np.exp2(scales.astype(np.float64) - 127.0), 8, axis=1)[..., None]
    return vals.transpose(0, 1, 3, 2).reshape(g * 512, n)

def pack4(w):
    words, scales = pack_weight(w, "e2m1")
    return words.reshape(words.shape[0], 128, -1), scales


def unpack4(words, scales):
    return unpack_weight(words.reshape(words.shape[0], 128, -1, 2), scales, "e2m1")


def kspread(k):
    return np.exp2(np.repeat(np.random.randint(-6, 7, k // 32), 32).astype(np.float64))


B, S, H, K, D, HID, WIN, QB = 1, 1536, 8, 2, 128, 2048, 512, 512
T = B * S
NQKV = (H + 2 * K) * D


def rope(x, cos, sin):
    x1, x2 = np.split(x, 2, axis=-1)
    return np.concatenate([x1 * cos - x2 * sin, x2 * cos + x1 * sin], axis=-1)


def setup_inputs():
    s = kspread(HID)
    ang = np.random.uniform(-np.pi, np.pi, (T, HID // HID * D // 2))
    hidden_states = np.random.standard_normal((T, HID)) * s
    hidden_states_words, hidden_states_scales = pack4(np.ascontiguousarray(hidden_states.T))
    w = np.random.standard_normal((NQKV, HID)) * 1.25 / np.sqrt(HID) / s[None, :]
    words, scales = pack4(np.ascontiguousarray(w.T))
    qkv_b = bf(np.random.standard_normal(NQKV) * 0.3)
    return {"hidden_states_words": hidden_states_words, "hidden_states_scales": hidden_states_scales,
            "cos": bf(np.cos(ang)), "sin": bf(np.sin(ang)),
            "qkv_w_words": words, "qkv_w_scales": scales,
            "qkv_b": qkv_b}


def reference(hidden_states_words, hidden_states_scales, cos, sin, qkv_w_words, qkv_w_scales, qkv_b):
    qkv = (unpack4(hidden_states_words, hidden_states_scales).T @ unpack4(qkv_w_words, qkv_w_scales)) + f64(qkv_b)
    q = qkv[:, : H * D].reshape(B, S, H, D)
    k = qkv[:, H * D : (H + K) * D].reshape(B, S, K, D)
    v = qkv[:, (H + K) * D :].reshape(B, S, K, D)
    c = f64(cos).reshape(B, S, 1, D // 2)
    s = f64(sin).reshape(B, S, 1, D // 2)
    return rope(q, c, s), rope(k, c, s), v

@@ -1,0 +1,234 @@
+from contextlib import ExitStack
+
+import concourse.mybir as mybir
+from concourse.masks import make_identity
+
+F32 = mybir.dt.float32
+BF16 = mybir.dt.bfloat16
+I32 = mybir.dt.int32
+U8 = mybir.dt.uint8
+FP4X4 = mybir.dt.float4_e2m1fn_x4
+ADD = mybir.AluOpType.add
+MULT = mybir.AluOpType.mult
+IDENTITY = mybir.ActivationFunctionType.Identity
+
+P = 128
+TOKENS = 1536
+HIDDEN = 2048
+HEADS = 8
+KV = 2
+D = 128
+HALF = 64
+COLS = (HEADS + 2 * KV) * D
+PASSES = HIDDEN // 512
+CHUNK = 512
+NCHUNK = TOKENS // CHUNK
+JB = CHUNK // P
+NQ = HEADS * NCHUNK
+NKV = TOKENS // P
+
+FLOPS = 2 * TOKENS * HIDDEN * COLS
+
+
+def tile_starcoder2attention_pa_kernel(tc, x_words, x_scales, cos, sin, w_words, w_scales, bias, out_q, out_k, out_v):
+    nc = tc.nc
+    with ExitStack() as ctx:
+        ctx.enter_context(tc.manual_schedule())
+        keep = ctx.enter_context(tc.tile_pool(name="keep", bufs=1))
+        work = ctx.enter_context(tc.tile_pool(name="work", bufs=4))
+        psum = ctx.enter_context(tc.psum_pool(name="psum", bufs=3))
+
+        def code_tile(name, width):
+            return keep.tile([P, PASSES, 2 * width], U8, name=name, align_bytes=64)
+
+        def scale_tile(name, width):
+            return keep.tile([P, PASSES, width], U8, name=name, align_bytes=64)
+
+        xa, wa = code_tile("xa", CHUNK), code_tile("wa", CHUNK)
+        xb, wb = code_tile("xb", 2 * CHUNK), code_tile("wb", 2 * CHUNK)
+        xsa, wsa = scale_tile("xsa", CHUNK), scale_tile("wsa", CHUNK)
+        xsb, wsb = scale_tile("xsb", 2 * CHUNK), scale_tile("wsb", 2 * CHUNK)
+
+        def load_codes(tile, src, c0, width):
+            nc.sync.dma_start(
+                out=tile[:].bitcast(I32),
+                in_=src[:, :, 2 * c0 : 2 * (c0 + width)].rearrange("g p c -> p g c").bitcast(I32),
+            )
+
+        def load_scales(tile, src, c0, width):
+            for q in range(4):
+                nc.sync.dma_start(
+                    out=tile[32 * q : 32 * q + 4, :, :].bitcast(I32),
+                    in_=src[:, 4 * q : 4 * q + 4, c0 : c0 + width].rearrange("g r n -> r g n").bitcast(I32),
+                )
+
+        bias_rows = keep.tile([P, P], BF16, name="bias_rows")
+        nc.vector.memset(bias_rows[:], 0.0)
+        nc.vector.memset(xsa[:].bitcast(I32), 0)
+        nc.vector.memset(wsa[:].bitcast(I32), 0)
+        nc.vector.memset(wsb[:].bitcast(I32), 0)
+        nc.vector.memset(xsb[:].bitcast(I32), 0)
+
+        load_codes(xa, x_words, 0, CHUNK)
+        load_codes(wa, w_words, 0, CHUNK)
+        load_scales(xsa, x_scales, 0, CHUNK)
+        load_scales(wsa, w_scales, 0, CHUNK)
+        load_codes(wb, w_words, CHUNK, 2 * CHUNK)
+        load_scales(wsb, w_scales, CHUNK, 2 * CHUNK)
+        load_codes(xb, x_words, CHUNK, 2 * CHUNK)
+        load_scales(xsb, x_scales, CHUNK, 2 * CHUNK)
+
+        ident_bf = keep.tile([P, P], BF16, name="ident_bf")
+        ident = keep.tile([P, P], F32, name="ident")
+        nc.gpsimd.dma_start(out=bias_rows[0 : COLS // P, :], in_=bias.rearrange("(a b) -> a b", b=P))
+        make_identity(nc, ident_bf[:])
+        make_identity(nc, ident[:])
+
+        cs = []
+        for c in range(NCHUNK):
+            t = keep.tile([P, 2, JB, D], BF16, name="cs%d" % c)
+            cs.append(t)
+            for f, src in ((0, cos), (1, sin)):
+                nc.gpsimd.dma_start(
+                    out=t[:, f, :, 0:HALF],
+                    in_=src[c * CHUNK : (c + 1) * CHUNK, :].rearrange("(j p) i -> p j i", p=P),
+                )
+
+        bt_ps = psum.tile([P, P], BF16, name="bt_ps", tag="kv", bufs=2)
+        nc.tensor.transpose(bt_ps[:], bias_rows[:], ident_bf[:])
+        bias_bf = keep.tile([P, 2 * KV + HEADS], BF16, name="bias_bf")
+        nc.scalar.copy(out=bias_bf[:], in_=bt_ps[:, 0 : COLS // P])
+        bias_col = keep.tile([P, COLS // P], F32, name="bias_col")
+        nc.scalar.copy(out=bias_col[:], in_=bt_ps[:, 0 : COLS // P])
+        kvb_ps = psum.tile([P, CHUNK], F32, name="kvb_ps", tag="kv", bufs=2)
+        for b in range(2 * KV):
+            nc.tensor.matmul(
+                kvb_ps[:, b * P : (b + 1) * P],
+                lhsT=bias_bf[:, HEADS + b : HEADS + b + 1].to_broadcast([P, P]),
+                rhs=ident_bf[:],
+                start=True,
+                stop=True,
+            )
+        kv_bias = keep.tile([P, CHUNK], F32, name="kv_bias")
+        nc.scalar.copy(out=kv_bias[:], in_=kvb_ps[:])
+
+        def prepare_cs(c):
+            nc.scalar.copy(out=cs[c][:, 0, :, HALF:D], in_=cs[c][:, 0, :, 0:HALF])
+            nc.scalar.mul(out=cs[c][:, 1, :, HALF:D], in_=cs[c][:, 1, :, 0:HALF], mul=-1.0)
+
+        prepare_cs(0)
+
+        def x_at(g, t0, width):
+            tile, stile, base = (xa, xsa, 0) if t0 < CHUNK else (xb, xsb, CHUNK)
+            a = t0 - base
+            return tile[:, g, 2 * a : 2 * (a + width)].bitcast(FP4X4), stile[:, g, a : a + width]
+
+        def w_at(g, c0, width):
+            tile, stile, base = (wa, wsa, 0) if c0 < CHUNK else (wb, wsb, CHUNK)
+            a = c0 - base
+            return tile[:, g, 2 * a : 2 * (a + width)].bitcast(FP4X4), stile[:, g, a : a + width]
+
+        ys, qouts = {}, {}
+
+        def query_matmul(n):
+            c, h = n // HEADS, n % HEADS
+            acc = psum.tile([P, CHUNK], F32, name="acc", tag="q", bufs=3)
+            for g in range(PASSES):
+                wv, wsv = w_at(g, h * D, D)
+                xv, xsv = x_at(g, c * CHUNK, CHUNK)
+                nc.tensor.matmul_mx(out=acc[:], lhsT=wv, lhsT_scale=wsv, rhs=xv, rhs_scale=xsv, start=(g == 0), stop=(g == PASSES - 1))
+            y = work.tile([P, CHUNK], F32, name="y")
+            nc.scalar.activation(out=y[:], in_=acc[:], func=IDENTITY, bias=bias_col[:, h : h + 1])
+            ys[n] = y
+
+        def query_turn(n):
+            y = ys.pop(n)
+            tb = psum.tile([P, CHUNK], F32, name="tb", tag="t", bufs=3)
+            for j in range(JB):
+                nc.tensor.transpose(tb[:, j * P : (j + 1) * P], y[:, j * P : (j + 1) * P], ident[:])
+            return tb
+
+        def query_products(n, tb):
+            c = n // HEADS
+            m = work.tile([P, 2, CHUNK], F32, name="m")
+            nc.vector.tensor_tensor(
+                out=m[:],
+                in0=tb[:].unsqueeze(1).to_broadcast([P, 2, CHUNK]),
+                in1=cs[c][:].rearrange("p f j d -> p f (j d)"),
+                op=MULT,
+            )
+            return m
+
+        def query_sum(n, m):
+            c, h = n // HEADS, n % HEADS
+            if h % 2 == 0:
+                qouts[n // 2] = work.tile([P, JB, 2, D], F32, name="qo")
+            o = qouts[n // 2]
+            nc.gpsimd.tensor_tensor(
+                out=o[:, :, h % 2, :].rearrange("p j (a i) -> p j a i", a=2),
+                in0=m[:, 0, :].rearrange("p (j a i) -> p j a i", a=2, i=HALF),
+                in1=m[:, 1, :].rearrange("p (j a i) -> p j a i", a=2, i=HALF)[:, :, ::-1, :],
+                op=ADD,
+            )
+            if h % 2 == 1:
+                nc.sync.dma_start(
+                    out=out_q[0, c * CHUNK : (c + 1) * CHUNK, h - 1 : h + 1, :].rearrange("(j p) h d -> p j h d", p=P),
+                    in_=o[:],
+                )
+
+        def kv_matmul(t):
+            acc = psum.tile([P, CHUNK], F32, name="kacc", tag="kv", bufs=2)
+            for g in range(PASSES):
+                xv, xsv = x_at(g, t * P, P)
+                wv, wsv = w_at(g, HEADS * D, CHUNK)
+                nc.tensor.matmul_mx(out=acc[:], lhsT=xv, lhsT_scale=xsv, rhs=wv, rhs_scale=wsv, start=(g == 0), stop=(g == PASSES - 1))
+            return acc
+
+        def kv_bias_add(t, acc):
+            kv = work.tile([P, 2 * KV, D], F32, name="kv")
+            nc.vector.tensor_tensor(out=kv[:].rearrange("p h d -> p (h d)"), in0=acc[:], in1=kv_bias[:], op=ADD)
+            nc.sync.dma_start(out=out_v[0, t * P : (t + 1) * P, :, :], in_=kv[:, KV : 2 * KV, :])
+            return kv
+
+        def key_products(t, kv):
+            mk = work.tile([P, 2, KV * D], F32, name="mk")
+            nc.vector.tensor_tensor(
+                out=mk[:].rearrange("p f (h d) -> p f h d", d=D),
+                in0=kv[:, 0:KV, :].unsqueeze(1).to_broadcast([P, 2, KV, D]),
+                in1=cs[t // JB][:, :, t % JB, :].unsqueeze(2).to_broadcast([P, 2, KV, D]),
+                op=MULT,
+            )
+            return mk
+
+        def key_sum(t, mk):
+            ko = work.tile([P, KV, D], F32, name="ko")
+            nc.gpsimd.tensor_tensor(
+                out=ko[:].rearrange("p h (a i) -> p h a i", a=2),
+                in0=mk[:, 0, :].rearrange("p (h a i) -> p h a i", a=2, i=HALF),
+                in1=mk[:, 1, :].rearrange("p (h a i) -> p h a i", a=2, i=HALF)[:, :, ::-1, :],
+                op=ADD,
+            )
+            nc.sync.dma_start(out=out_k[0, t * P : (t + 1) * P, :, :], in_=ko[:])
+
+        query_matmul(0)
+        for i in range(NQ // 2):
+            t = i - 2
+            for n in (2 * i + 1, 2 * i + 2):
+                if n < NQ:
+                    query_matmul(n)
+            if i in (1, 4):
+                prepare_cs((i + 2) // 3)
+            kacc = kv_matmul(t) if t >= 0 else None
+            tb0 = query_turn(2 * i)
+            tb1 = query_turn(2 * i + 1)
+            kv = kv_bias_add(t, kacc) if t >= 0 else None
+            m0 = query_products(2 * i, tb0)
+            mk = key_products(t, kv) if t >= 0 else None
+            m1 = query_products(2 * i + 1, tb1)
+            query_sum(2 * i, m0)
+            query_sum(2 * i + 1, m1)
+            if t >= 0:
+                key_sum(t, mk)
+        for t in (NKV - 2, NKV - 1):
+            kacc = kv_matmul(t)
+            key_sum(t, key_products(t, kv_bias_add(t, kacc)))

@@ -20,12 +20,12 @@ KV = 2
 D = 128
 HALF = 64
 COLS = (HEADS + 2 * KV) * D
+BLOCKS = COLS // P
 PASSES = HIDDEN // 512
 CHUNK = 512
 NCHUNK = TOKENS // CHUNK
 JB = CHUNK // P
-NQ = HEADS * NCHUNK
-NKV = TOKENS // P
+FIRST = 4
 
 FLOPS = 2 * TOKENS * HIDDEN * COLS
 
@@ -36,7 +36,7 @@ def tile_starcoder2attention_pa_kernel(tc, x_words, x_scales, cos, sin, w_words,
         ctx.enter_context(tc.manual_schedule())
         keep = ctx.enter_context(tc.tile_pool(name="keep", bufs=1))
         work = ctx.enter_context(tc.tile_pool(name="work", bufs=4))
-        psum = ctx.enter_context(tc.psum_pool(name="psum", bufs=3))
+        psum = ctx.enter_context(tc.psum_pool(name="psum", bufs=2))
 
         def code_tile(name, width):
             return keep.tile([P, PASSES, 2 * width], U8, name=name, align_bytes=64)
@@ -44,15 +44,16 @@ def tile_starcoder2attention_pa_kernel(tc, x_words, x_scales, cos, sin, w_words,
         def scale_tile(name, width):
             return keep.tile([P, PASSES, width], U8, name=name, align_bytes=64)
 
+        x0 = code_tile("x0", P)
         xa, wa = code_tile("xa", CHUNK), code_tile("wa", CHUNK)
         xb, wb = code_tile("xb", 2 * CHUNK), code_tile("wb", 2 * CHUNK)
         xsa, wsa = scale_tile("xsa", CHUNK), scale_tile("wsa", CHUNK)
         xsb, wsb = scale_tile("xsb", 2 * CHUNK), scale_tile("wsb", 2 * CHUNK)
 
-        def load_codes(tile, src, c0, width):
+        def load_codes(tile, src, c0, width, g0=0, g1=PASSES):
             nc.sync.dma_start(
-                out=tile[:].bitcast(I32),
-                in_=src[:, :, 2 * c0 : 2 * (c0 + width)].rearrange("g p c -> p g c").bitcast(I32),
+                out=tile[:, g0:g1, :].bitcast(I32),
+                in_=src[g0:g1, :, 2 * c0 : 2 * (c0 + width)].rearrange("g p c -> p g c").bitcast(I32),
             )
 
         def load_scales(tile, src, c0, width):
@@ -63,16 +64,20 @@ def tile_starcoder2attention_pa_kernel(tc, x_words, x_scales, cos, sin, w_words,
                 )
 
         bias_rows = keep.tile([P, P], BF16, name="bias_rows")
+        warm = keep.tile([P, P], BF16, name="warm")
         nc.vector.memset(bias_rows[:], 0.0)
+        nc.vector.memset(warm[:], 0.0)
         nc.vector.memset(xsa[:].bitcast(I32), 0)
-        nc.vector.memset(wsa[:].bitcast(I32), 0)
+        nc.gpsimd.memset(wsa[:].bitcast(I32), 0)
         nc.vector.memset(wsb[:].bitcast(I32), 0)
         nc.vector.memset(xsb[:].bitcast(I32), 0)
 
-        load_codes(xa, x_words, 0, CHUNK)
-        load_codes(wa, w_words, 0, CHUNK)
+        load_codes(x0, x_words, 0, P)
+        load_codes(wa, w_words, 0, CHUNK, 0, 2)
         load_scales(xsa, x_scales, 0, CHUNK)
         load_scales(wsa, w_scales, 0, CHUNK)
+        load_codes(wa, w_words, 0, CHUNK, 2, 4)
+        load_codes(xa, x_words, 0, CHUNK)
         load_codes(wb, w_words, CHUNK, 2 * CHUNK)
         load_scales(wsb, w_scales, CHUNK, 2 * CHUNK)
         load_codes(xb, x_words, CHUNK, 2 * CHUNK)
@@ -80,155 +85,167 @@ def tile_starcoder2attention_pa_kernel(tc, x_words, x_scales, cos, sin, w_words,
 
         ident_bf = keep.tile([P, P], BF16, name="ident_bf")
         ident = keep.tile([P, P], F32, name="ident")
-        nc.gpsimd.dma_start(out=bias_rows[0 : COLS // P, :], in_=bias.rearrange("(a b) -> a b", b=P))
+        nc.gpsimd.dma_start(out=bias_rows[0:BLOCKS, :], in_=bias.rearrange("(a b) -> a b", b=P))
         make_identity(nc, ident_bf[:])
-        make_identity(nc, ident[:])
 
-        cs = []
-        for c in range(NCHUNK):
-            t = keep.tile([P, 2, JB, D], BF16, name="cs%d" % c)
-            cs.append(t)
+        csa = keep.tile([P, 2, JB, D], BF16, name="csa")
+        csb = keep.tile([P, 2, 2 * JB, D], BF16, name="csb")
+
+        def load_cs(tile, t0, t1):
             for f, src in ((0, cos), (1, sin)):
-                nc.gpsimd.dma_start(
-                    out=t[:, f, :, 0:HALF],
-                    in_=src[c * CHUNK : (c + 1) * CHUNK, :].rearrange("(j p) i -> p j i", p=P),
-                )
+                nc.gpsimd.dma_start(out=tile[:, f, :, 0:HALF], in_=src[t0:t1, :].rearrange("(j p) i -> p j i", p=P))
 
-        bt_ps = psum.tile([P, P], BF16, name="bt_ps", tag="kv", bufs=2)
+        def prepare_cs(tile):
+            nc.scalar.copy(out=tile[:, 0, :, HALF:D], in_=tile[:, 0, :, 0:HALF])
+            nc.scalar.mul(out=tile[:, 1, :, HALF:D], in_=tile[:, 1, :, 0:HALF], mul=-1.0)
+
+        def cs_at(t, n):
+            return csa[:, :, t : t + n, :] if t < JB else csb[:, :, t - JB : t - JB + n, :]
+
+        load_cs(csa, 0, CHUNK)
+        make_identity(nc, ident[:])
+        load_cs(csb, CHUNK, TOKENS)
+
+        warm_ps = psum.tile([P, CHUNK], F32, name="warm_ps", tag="t", bufs=3)
+
+        def warm_up(count):
+            for unused in range(count):
+                nc.tensor.matmul(warm_ps[:], lhsT=warm[:], rhs=warm[:, 0:1].to_broadcast([P, CHUNK]), start=True, stop=True)
+
+        warm_up(7)
+        bt_ps = psum.tile([P, P], BF16, name="bt_ps", tag="kv", bufs=3)
         nc.tensor.transpose(bt_ps[:], bias_rows[:], ident_bf[:])
-        bias_bf = keep.tile([P, 2 * KV + HEADS], BF16, name="bias_bf")
-        nc.scalar.copy(out=bias_bf[:], in_=bt_ps[:, 0 : COLS // P])
-        bias_col = keep.tile([P, COLS // P], F32, name="bias_col")
-        nc.scalar.copy(out=bias_col[:], in_=bt_ps[:, 0 : COLS // P])
-        kvb_ps = psum.tile([P, CHUNK], F32, name="kvb_ps", tag="kv", bufs=2)
-        for b in range(2 * KV):
-            nc.tensor.matmul(
-                kvb_ps[:, b * P : (b + 1) * P],
-                lhsT=bias_bf[:, HEADS + b : HEADS + b + 1].to_broadcast([P, P]),
-                rhs=ident_bf[:],
-                start=True,
-                stop=True,
-            )
-        kv_bias = keep.tile([P, CHUNK], F32, name="kv_bias")
-        nc.scalar.copy(out=kv_bias[:], in_=kvb_ps[:])
+        bias_bf = keep.tile([P, BLOCKS], BF16, name="bias_bf")
+        nc.scalar.copy(out=bias_bf[:], in_=bt_ps[:, 0:BLOCKS])
+        bias_col = keep.tile([P, BLOCKS], F32, name="bias_col")
+        nc.scalar.copy(out=bias_col[:], in_=bt_ps[:, 0:BLOCKS])
 
-        def prepare_cs(c):
-            nc.scalar.copy(out=cs[c][:, 0, :, HALF:D], in_=cs[c][:, 0, :, 0:HALF])
-            nc.scalar.mul(out=cs[c][:, 1, :, HALF:D], in_=cs[c][:, 1, :, 0:HALF], mul=-1.0)
+        def spread_bias(blocks, name):
+            ps = psum.tile([P, CHUNK], F32, name=name + "_ps", tag="q", bufs=2)
+            row = keep.tile([P, len(blocks) * P], F32, name=name)
+            for i in range(len(blocks)):
+                b = blocks[i]
+                nc.tensor.matmul(ps[:, i * P : (i + 1) * P], lhsT=bias_bf[:, b : b + 1].to_broadcast([P, P]), rhs=ident_bf[:], start=True, stop=True)
+            nc.scalar.copy(out=row[:], in_=ps[:, 0 : len(blocks) * P])
+            return row
 
-        prepare_cs(0)
+        first_bias = spread_bias(tuple(range(FIRST)), "first_bias")
+        value_bias = spread_bias((BLOCKS - 2, BLOCKS - 1), "value_bias")
+        warm_up(3)
+        prepare_cs(csa)
 
-        def x_at(g, t0, width):
-            tile, stile, base = (xa, xsa, 0) if t0 < CHUNK else (xb, xsb, CHUNK)
-            a = t0 - base
-            return tile[:, g, 2 * a : 2 * (a + width)].bitcast(FP4X4), stile[:, g, a : a + width]
-
-        def w_at(g, c0, width):
-            tile, stile, base = (wa, wsa, 0) if c0 < CHUNK else (wb, wsb, CHUNK)
+        def part(pair, g, c0, width):
+            tile, stile, base = pair
             a = c0 - base
             return tile[:, g, 2 * a : 2 * (a + width)].bitcast(FP4X4), stile[:, g, a : a + width]
 
-        ys, qouts = {}, {}
+        def x_at(g, t0, width):
+            if t0 == 0 and width == P:
+                return x0[:, g, :].bitcast(FP4X4), xsa[:, g, 0:P]
+            return part((xa, xsa, 0) if t0 < CHUNK else (xb, xsb, CHUNK), g, t0, width)
 
-        def query_matmul(n):
-            c, h = n // HEADS, n % HEADS
-            acc = psum.tile([P, CHUNK], F32, name="acc", tag="q", bufs=3)
+        def w_at(g, c0, width):
+            return part((wa, wsa, 0) if c0 < CHUNK else (wb, wsb, CHUNK), g, c0, width)
+
+        def tokens_matmul(out, t0, c0, width):
+            for g in range(PASSES):
+                xv, xsv = x_at(g, t0, P)
+                wv, wsv = w_at(g, c0, width)
+                nc.tensor.matmul_mx(out=out, lhsT=xv, lhsT_scale=xsv, rhs=wv, rhs_scale=wsv, start=(g == 0), stop=(g == PASSES - 1))
+
+        def add_turned(out, m):
+            nc.gpsimd.tensor_tensor(
+                out=out.rearrange("p x (a i) -> p x a i", a=2),
+                in0=m[:, 0, :].rearrange("p (x a i) -> p x a i", a=2, i=HALF),
+                in1=m[:, 1, :].rearrange("p (x a i) -> p x a i", a=2, i=HALF)[:, :, ::-1, :],
+                op=ADD,
+            )
+
+        def first_block(t):
+            acc = psum.tile([P, CHUNK], F32, name="facc", tag="kv", bufs=3)
+            tokens_matmul(acc[:], t * P, 0, CHUNK)
+            y = work.tile([P, FIRST, D], F32, name="fy")
+            nc.vector.tensor_tensor(out=y[:].rearrange("p h d -> p (h d)"), in0=acc[:], in1=first_bias[:], op=ADD)
+            m = work.tile([P, 2, CHUNK], F32, name="m")
+            nc.vector.tensor_tensor(
+                out=m[:].rearrange("p f (h d) -> p f h d", d=D),
+                in0=y[:].unsqueeze(1).to_broadcast([P, 2, FIRST, D]),
+                in1=cs_at(t, 1)[:, :, 0, :].unsqueeze(2).to_broadcast([P, 2, FIRST, D]),
+                op=MULT,
+            )
+            o = work.tile([P, FIRST, D], F32, name="fo")
+            add_turned(o[:], m)
+            nc.sync.dma_start(out=out_q[0, t * P : (t + 1) * P, 0:FIRST, :], in_=o[:])
+
+        units = [(c, h) for c in range(NCHUNK) for h in range(HEADS + KV) if c > 0 or h >= FIRST]
+        ys, pairs = {}, {}
+
+        def unit_matmul(n):
+            c, h = units[n]
+            acc = psum.tile([P, CHUNK], F32, name="acc", tag="q", bufs=2)
             for g in range(PASSES):
                 wv, wsv = w_at(g, h * D, D)
                 xv, xsv = x_at(g, c * CHUNK, CHUNK)
                 nc.tensor.matmul_mx(out=acc[:], lhsT=wv, lhsT_scale=wsv, rhs=xv, rhs_scale=xsv, start=(g == 0), stop=(g == PASSES - 1))
-            y = work.tile([P, CHUNK], F32, name="y")
-            nc.scalar.activation(out=y[:], in_=acc[:], func=IDENTITY, bias=bias_col[:, h : h + 1])
-            ys[n] = y
+            ys[n] = work.tile([P, CHUNK], F32, name="y", bufs=6)
+            nc.scalar.activation(out=ys[n][:], in_=acc[:], func=IDENTITY, bias=bias_col[:, h : h + 1])
 
-        def query_turn(n):
-            y = ys.pop(n)
+        def unit_turn(n):
             tb = psum.tile([P, CHUNK], F32, name="tb", tag="t", bufs=3)
             for j in range(JB):
-                nc.tensor.transpose(tb[:, j * P : (j + 1) * P], y[:, j * P : (j + 1) * P], ident[:])
+                nc.tensor.transpose(tb[:, j * P : (j + 1) * P], ys[n][:, j * P : (j + 1) * P], ident[:])
             return tb
 
-        def query_products(n, tb):
-            c = n // HEADS
+        def unit_rope(n, tb):
+            c, h = units[n]
             m = work.tile([P, 2, CHUNK], F32, name="m")
             nc.vector.tensor_tensor(
                 out=m[:],
                 in0=tb[:].unsqueeze(1).to_broadcast([P, 2, CHUNK]),
-                in1=cs[c][:].rearrange("p f j d -> p f (j d)"),
+                in1=cs_at(c * JB, JB).rearrange("p f j d -> p f (j d)"),
                 op=MULT,
             )
-            return m
-
-        def query_sum(n, m):
-            c, h = n // HEADS, n % HEADS
-            if h % 2 == 0:
-                qouts[n // 2] = work.tile([P, JB, 2, D], F32, name="qo")
-            o = qouts[n // 2]
-            nc.gpsimd.tensor_tensor(
-                out=o[:, :, h % 2, :].rearrange("p j (a i) -> p j a i", a=2),
-                in0=m[:, 0, :].rearrange("p (j a i) -> p j a i", a=2, i=HALF),
-                in1=m[:, 1, :].rearrange("p (j a i) -> p j a i", a=2, i=HALF)[:, :, ::-1, :],
-                op=ADD,
-            )
-            if h % 2 == 1:
+            if n % 2 == 0:
+                pairs[n // 2] = work.tile([P, JB, 2, D], F32, name="pair")
+            o = pairs[n // 2]
+            add_turned(o[:, :, n % 2, :], m)
+            if n % 2 == 1:
+                dst, h0 = (out_q, h - 1) if h < HEADS else (out_k, h - 1 - HEADS)
                 nc.sync.dma_start(
-                    out=out_q[0, c * CHUNK : (c + 1) * CHUNK, h - 1 : h + 1, :].rearrange("(j p) h d -> p j h d", p=P),
-                    in_=o[:],
+                    out=dst[0, c * CHUNK : (c + 1) * CHUNK, h0 : h0 + 2, :].rearrange("(j p) h d -> p j h d", p=P), in_=o[:]
                 )
 
-        def kv_matmul(t):
-            acc = psum.tile([P, CHUNK], F32, name="kacc", tag="kv", bufs=2)
-            for g in range(PASSES):
-                xv, xsv = x_at(g, t * P, P)
-                wv, wsv = w_at(g, HEADS * D, CHUNK)
-                nc.tensor.matmul_mx(out=acc[:], lhsT=xv, lhsT_scale=xsv, rhs=wv, rhs_scale=wsv, start=(g == 0), stop=(g == PASSES - 1))
+        def value_matmul(b):
+            acc = psum.tile([P, 2, KV * D], F32, name="vacc", tag="kv", bufs=3)
+            for j in range(2):
+                tokens_matmul(acc[:, j, :], (2 * b + j) * P, (HEADS + KV) * D, KV * D)
             return acc
 
-        def kv_bias_add(t, acc):
-            kv = work.tile([P, 2 * KV, D], F32, name="kv")
-            nc.vector.tensor_tensor(out=kv[:].rearrange("p h d -> p (h d)"), in0=acc[:], in1=kv_bias[:], op=ADD)
-            nc.sync.dma_start(out=out_v[0, t * P : (t + 1) * P, :, :], in_=kv[:, KV : 2 * KV, :])
-            return kv
-
-        def key_products(t, kv):
-            mk = work.tile([P, 2, KV * D], F32, name="mk")
-            nc.vector.tensor_tensor(
-                out=mk[:].rearrange("p f (h d) -> p f h d", d=D),
-                in0=kv[:, 0:KV, :].unsqueeze(1).to_broadcast([P, 2, KV, D]),
-                in1=cs[t // JB][:, :, t % JB, :].unsqueeze(2).to_broadcast([P, 2, KV, D]),
-                op=MULT,
+        def value_out(b, acc):
+            y = work.tile([P, 2, KV * D], F32, name="vo")
+            nc.vector.tensor_tensor(out=y[:], in0=acc[:], in1=value_bias[:].unsqueeze(1).to_broadcast([P, 2, KV * D]), op=ADD)
+            nc.sync.dma_start(
+                out=out_v[0, 2 * b * P : 2 * (b + 1) * P, :, :].rearrange("(j p) h d -> p j (h d)", p=P), in_=y[:]
             )
-            return mk
 
-        def key_sum(t, mk):
-            ko = work.tile([P, KV, D], F32, name="ko")
-            nc.gpsimd.tensor_tensor(
-                out=ko[:].rearrange("p h (a i) -> p h a i", a=2),
-                in0=mk[:, 0, :].rearrange("p (h a i) -> p h a i", a=2, i=HALF),
-                in1=mk[:, 1, :].rearrange("p (h a i) -> p h a i", a=2, i=HALF)[:, :, ::-1, :],
-                op=ADD,
-            )
-            nc.sync.dma_start(out=out_k[0, t * P : (t + 1) * P, :, :], in_=ko[:])
-
-        query_matmul(0)
-        for i in range(NQ // 2):
-            t = i - 2
-            for n in (2 * i + 1, 2 * i + 2):
-                if n < NQ:
-                    query_matmul(n)
-            if i in (1, 4):
-                prepare_cs((i + 2) // 3)
-            kacc = kv_matmul(t) if t >= 0 else None
-            tb0 = query_turn(2 * i)
-            tb1 = query_turn(2 * i + 1)
-            kv = kv_bias_add(t, kacc) if t >= 0 else None
-            m0 = query_products(2 * i, tb0)
-            mk = key_products(t, kv) if t >= 0 else None
-            m1 = query_products(2 * i + 1, tb1)
-            query_sum(2 * i, m0)
-            query_sum(2 * i + 1, m1)
-            if t >= 0:
-                key_sum(t, mk)
-        for t in (NKV - 2, NKV - 1):
-            kacc = kv_matmul(t)
-            key_sum(t, key_products(t, kv_bias_add(t, kacc)))
+        for t in range(JB):
+            first_block(t)
+        sizes = (2, 3, 3, 3, 3, 3, 3, 3, 3)
+        extra = {4: 0, 6: 1}
+        made = turned = 0
+        for i in range(len(sizes)):
+            group = range(turned, turned + sizes[i])
+            turned += sizes[i]
+            while made < min(turned + 1, len(units)):
+                unit_matmul(made)
+                made += 1
+            if i == 0:
+                prepare_cs(csb)
+            vacc = value_matmul(extra[i]) if i in extra else None
+            tbs = [unit_turn(n) for n in group]
+            if i in extra:
+                value_out(extra[i], vacc)
+            for n in group:
+                unit_rope(n, tbs[n - group.start])
+        for b in (2, 3, 4, 5):
+            value_out(b, value_matmul(b))

@@ -25,6 +25,7 @@ PASSES = HIDDEN // 512
 CHUNK = 512
 NCHUNK = TOKENS // CHUNK
 JB = CHUNK // P
+MIDDLE = COLS - CHUNK - KV * D
 FIRST = 4
 
 FLOPS = 2 * TOKENS * HIDDEN * COLS
@@ -44,11 +45,10 @@ def tile_starcoder2attention_pa_kernel(tc, x_words, x_scales, cos, sin, w_words,
         def scale_tile(name, width):
             return keep.tile([P, PASSES, width], U8, name=name, align_bytes=64)
 
-        x0 = code_tile("x0", P)
         xa, wa = code_tile("xa", CHUNK), code_tile("wa", CHUNK)
-        xb, wb = code_tile("xb", 2 * CHUNK), code_tile("wb", 2 * CHUNK)
+        xb, wb, wv = code_tile("xb", 2 * CHUNK), code_tile("wb", MIDDLE), code_tile("wv", KV * D)
         xsa, wsa = scale_tile("xsa", CHUNK), scale_tile("wsa", CHUNK)
-        xsb, wsb = scale_tile("xsb", 2 * CHUNK), scale_tile("wsb", 2 * CHUNK)
+        xsb, wsb, wsv = scale_tile("xsb", 2 * CHUNK), scale_tile("wsb", MIDDLE), scale_tile("wsv", KV * D)
 
         def load_codes(tile, src, c0, width, g0=0, g1=PASSES):
             nc.sync.dma_start(
@@ -71,40 +71,41 @@ def tile_starcoder2attention_pa_kernel(tc, x_words, x_scales, cos, sin, w_words,
         nc.gpsimd.memset(wsa[:].bitcast(I32), 0)
         nc.vector.memset(wsb[:].bitcast(I32), 0)
         nc.vector.memset(xsb[:].bitcast(I32), 0)
+        nc.vector.memset(wsv[:].bitcast(I32), 0)
 
-        load_codes(x0, x_words, 0, P)
+        load_codes(xa, x_words, 0, CHUNK, 0, 2)
         load_codes(wa, w_words, 0, CHUNK, 0, 2)
         load_scales(xsa, x_scales, 0, CHUNK)
         load_scales(wsa, w_scales, 0, CHUNK)
+        load_codes(xa, x_words, 0, CHUNK, 2, 4)
         load_codes(wa, w_words, 0, CHUNK, 2, 4)
-        load_codes(xa, x_words, 0, CHUNK)
-        load_codes(wb, w_words, CHUNK, 2 * CHUNK)
-        load_scales(wsb, w_scales, CHUNK, 2 * CHUNK)
+        angles = [keep.tile([P, 2, n, HALF], BF16, name="angles%d" % n) for n in (JB, TOKENS // P - JB)]
+        tables = [keep.tile([P, 2, n, D], BF16, name="cs%d" % n) for n in (JB, TOKENS // P - JB)]
+
+        def load_angles(k, t0, t1):
+            for f, src in ((0, cos), (1, sin)):
+                nc.scalar.dma_start(out=angles[k][:, f, :, :], in_=src[t0:t1, :].rearrange("(b p) i -> p b i", p=P))
+
+        def cs_at(b, n):
+            return tables[0][:, :, b : b + n, :] if b < JB else tables[1][:, :, b - JB : b - JB + n, :]
+
+        load_angles(0, 0, CHUNK)
+        load_codes(wb, w_words, CHUNK, MIDDLE)
+        load_scales(wsb, w_scales, CHUNK, MIDDLE)
         load_codes(xb, x_words, CHUNK, 2 * CHUNK)
         load_scales(xsb, x_scales, CHUNK, 2 * CHUNK)
+        load_codes(wv, w_words, CHUNK + MIDDLE, KV * D)
+        load_scales(wsv, w_scales, CHUNK + MIDDLE, KV * D)
+
+        def double(a):
+            return a.unsqueeze(2).to_broadcast([P, a.shape[1], 2, HALF])
 
         ident_bf = keep.tile([P, P], BF16, name="ident_bf")
         ident = keep.tile([P, P], F32, name="ident")
         nc.gpsimd.dma_start(out=bias_rows[0:BLOCKS, :], in_=bias.rearrange("(a b) -> a b", b=P))
         make_identity(nc, ident_bf[:])
 
-        csa = keep.tile([P, 2, JB, D], BF16, name="csa")
-        csb = keep.tile([P, 2, 2 * JB, D], BF16, name="csb")
-
-        def load_cs(tile, t0, t1):
-            for f, src in ((0, cos), (1, sin)):
-                nc.gpsimd.dma_start(out=tile[:, f, :, 0:HALF], in_=src[t0:t1, :].rearrange("(j p) i -> p j i", p=P))
-
-        def prepare_cs(tile):
-            nc.scalar.copy(out=tile[:, 0, :, HALF:D], in_=tile[:, 0, :, 0:HALF])
-            nc.scalar.mul(out=tile[:, 1, :, HALF:D], in_=tile[:, 1, :, 0:HALF], mul=-1.0)
-
-        def cs_at(t, n):
-            return csa[:, :, t : t + n, :] if t < JB else csb[:, :, t - JB : t - JB + n, :]
-
-        load_cs(csa, 0, CHUNK)
         make_identity(nc, ident[:])
-        load_cs(csb, CHUNK, TOKENS)
 
         warm_ps = psum.tile([P, CHUNK], F32, name="warm_ps", tag="t", bufs=3)
 
@@ -113,7 +114,7 @@ def tile_starcoder2attention_pa_kernel(tc, x_words, x_scales, cos, sin, w_words,
                 nc.tensor.matmul(warm_ps[:], lhsT=warm[:], rhs=warm[:, 0:1].to_broadcast([P, CHUNK]), start=True, stop=True)
 
         warm_up(7)
-        bt_ps = psum.tile([P, P], BF16, name="bt_ps", tag="kv", bufs=3)
+        bt_ps = psum.tile([P, P], BF16, name="bt_ps", tag="kv", bufs=2)
         nc.tensor.transpose(bt_ps[:], bias_rows[:], ident_bf[:])
         bias_bf = keep.tile([P, BLOCKS], BF16, name="bias_bf")
         nc.scalar.copy(out=bias_bf[:], in_=bt_ps[:, 0:BLOCKS])
@@ -129,10 +130,20 @@ def tile_starcoder2attention_pa_kernel(tc, x_words, x_scales, cos, sin, w_words,
             nc.scalar.copy(out=row[:], in_=ps[:, 0 : len(blocks) * P])
             return row
 
-        first_bias = spread_bias(tuple(range(FIRST)), "first_bias")
         value_bias = spread_bias((BLOCKS - 2, BLOCKS - 1), "value_bias")
+        first_bias = spread_bias(tuple(range(FIRST)), "first_bias")
         warm_up(3)
-        prepare_cs(csa)
+        cs, an = tables[0], angles[0]
+        nc.vector.tensor_copy(out=cs[:, 0, :, :].rearrange("p b (a i) -> p b a i", a=2), in_=double(an[:, 0, :, :]))
+        nc.vector.tensor_copy(out=cs[:, 1, :, 0:HALF], in_=an[:, 1, :, :])
+        nc.vector.tensor_scalar_mul(out=cs[:, 1, :, HALF:D], in0=an[:, 1, :, :], scalar1=-1.0)
+        load_angles(1, CHUNK, TOKENS)
+
+        def prepare_rest():
+            cs, an = tables[1], angles[1]
+            nc.scalar.copy(out=cs[:, 0, :, :].rearrange("p b (a i) -> p b a i", a=2), in_=double(an[:, 0, :, :]))
+            nc.scalar.copy(out=cs[:, 1, :, 0:HALF], in_=an[:, 1, :, :])
+            nc.scalar.mul(out=cs[:, 1, :, HALF:D], in_=an[:, 1, :, :], mul=-1.0)
 
         def part(pair, g, c0, width):
             tile, stile, base = pair
@@ -140,12 +151,12 @@ def tile_starcoder2attention_pa_kernel(tc, x_words, x_scales, cos, sin, w_words,
             return tile[:, g, 2 * a : 2 * (a + width)].bitcast(FP4X4), stile[:, g, a : a + width]
 
         def x_at(g, t0, width):
-            if t0 == 0 and width == P:
-                return x0[:, g, :].bitcast(FP4X4), xsa[:, g, 0:P]
             return part((xa, xsa, 0) if t0 < CHUNK else (xb, xsb, CHUNK), g, t0, width)
 
         def w_at(g, c0, width):
-            return part((wa, wsa, 0) if c0 < CHUNK else (wb, wsb, CHUNK), g, c0, width)
+            for last, pair in ((CHUNK, (wa, wsa, 0)), (CHUNK + MIDDLE, (wb, wsb, CHUNK)), (COLS, (wv, wsv, CHUNK + MIDDLE))):
+                if c0 < last:
+                    return part(pair, g, c0, width)
 
         def tokens_matmul(out, t0, c0, width):
             for g in range(PASSES):
@@ -161,23 +172,30 @@ def tile_starcoder2attention_pa_kernel(tc, x_words, x_scales, cos, sin, w_words,
                 op=ADD,
             )
 
-        def first_block(t):
-            acc = psum.tile([P, CHUNK], F32, name="facc", tag="kv", bufs=3)
-            tokens_matmul(acc[:], t * P, 0, CHUNK)
-            y = work.tile([P, FIRST, D], F32, name="fy")
-            nc.vector.tensor_tensor(out=y[:].rearrange("p h d -> p (h d)"), in0=acc[:], in1=first_bias[:], op=ADD)
-            m = work.tile([P, 2, CHUNK], F32, name="m")
-            nc.vector.tensor_tensor(
-                out=m[:].rearrange("p f (h d) -> p f h d", d=D),
-                in0=y[:].unsqueeze(1).to_broadcast([P, 2, FIRST, D]),
-                in1=cs_at(t, 1)[:, :, 0, :].unsqueeze(2).to_broadcast([P, 2, FIRST, D]),
-                op=MULT,
-            )
-            o = work.tile([P, FIRST, D], F32, name="fo")
-            add_turned(o[:], m)
-            nc.sync.dma_start(out=out_q[0, t * P : (t + 1) * P, 0:FIRST, :], in_=o[:])
+        def first_pair(b):
+            accs = [psum.tile([P, CHUNK], F32, name="facc", tag="kv", bufs=2) for j in range(2)]
+            plane = psum.tile([P, 2, 2, D], F32, name="plane", tag="plane", bufs=1)
+            tokens_matmul(accs[0][:], 2 * b * P, 0, CHUNK)
+            for j in range(2):
+                nc.tensor.matmul(plane[:, j, :, :], lhsT=ident_bf[:], rhs=cs_at(2 * b + j, 1)[:, :, 0, :], start=True, stop=True)
+            tokens_matmul(accs[1][:], (2 * b + 1) * P, 0, CHUNK)
+            rows = [work.tile([P, FIRST, D], F32, name="rows") for j in range(2)]
+            for j in range(2):
+                nc.vector.tensor_tensor(out=rows[j][:].rearrange("p h d -> p (h d)"), in0=accs[j][:], in1=first_bias[:], op=ADD)
+            for j in range(2):
+                t = 2 * b + j
+                m = work.tile([P, 2, CHUNK], F32, name="m", bufs=6)
+                nc.vector.tensor_tensor(
+                    out=m[:].rearrange("p f (h d) -> p f h d", d=D),
+                    in0=rows[j][:].unsqueeze(1).to_broadcast([P, 2, FIRST, D]),
+                    in1=plane[:, j, :, :].unsqueeze(2).to_broadcast([P, 2, FIRST, D]),
+                    op=MULT,
+                )
+                o = work.tile([P, FIRST, D], F32, name="fo")
+                add_turned(o[:], m)
+                nc.sync.dma_start(out=out_q[0, t * P : (t + 1) * P, 0:FIRST, :], in_=o[:])
 
-        units = [(c, h) for c in range(NCHUNK) for h in range(HEADS + KV) if c > 0 or h >= FIRST]
+        units = [(c, h) for c in range(NCHUNK) for h in range(FIRST, HEADS + KV)]
         ys, pairs = {}, {}
 
         def unit_matmul(n):
@@ -198,7 +216,7 @@ def tile_starcoder2attention_pa_kernel(tc, x_words, x_scales, cos, sin, w_words,
 
         def unit_rope(n, tb):
             c, h = units[n]
-            m = work.tile([P, 2, CHUNK], F32, name="m")
+            m = work.tile([P, 2, CHUNK], F32, name="m", bufs=6)
             nc.vector.tensor_tensor(
                 out=m[:],
                 in0=tb[:].unsqueeze(1).to_broadcast([P, 2, CHUNK]),
@@ -216,36 +234,34 @@ def tile_starcoder2attention_pa_kernel(tc, x_words, x_scales, cos, sin, w_words,
                 )
 
         def value_matmul(b):
-            acc = psum.tile([P, 2, KV * D], F32, name="vacc", tag="kv", bufs=3)
+            acc = psum.tile([P, 2, KV * D], F32, name="vacc", tag="kv", bufs=2)
             for j in range(2):
                 tokens_matmul(acc[:, j, :], (2 * b + j) * P, (HEADS + KV) * D, KV * D)
             return acc
 
-        def value_out(b, acc):
-            y = work.tile([P, 2, KV * D], F32, name="vo")
-            nc.vector.tensor_tensor(out=y[:], in0=acc[:], in1=value_bias[:].unsqueeze(1).to_broadcast([P, 2, KV * D]), op=ADD)
-            nc.sync.dma_start(
-                out=out_v[0, 2 * b * P : 2 * (b + 1) * P, :, :].rearrange("(j p) h d -> p j (h d)", p=P), in_=y[:]
-            )
+        def value_out(b, acc, step=2):
+            for j in range(0, 2, step):
+                y = work.tile([P, step, KV * D], F32, name="vo", bufs=6)
+                nc.vector.tensor_tensor(
+                    out=y[:], in0=acc[:, j : j + step, :], in1=value_bias[:].unsqueeze(1).to_broadcast([P, step, KV * D]), op=ADD
+                )
+                t0 = (2 * b + j) * P
+                nc.sync.dma_start(out=out_v[0, t0 : t0 + step * P, :, :].rearrange("(j p) h d -> p j (h d)", p=P), in_=y[:])
 
-        for t in range(JB):
-            first_block(t)
-        sizes = (2, 3, 3, 3, 3, 3, 3, 3, 3)
-        extra = {4: 0, 6: 1}
-        made = turned = 0
-        for i in range(len(sizes)):
-            group = range(turned, turned + sizes[i])
-            turned += sizes[i]
-            while made < min(turned + 1, len(units)):
-                unit_matmul(made)
-                made += 1
-            if i == 0:
-                prepare_cs(csb)
-            vacc = value_matmul(extra[i]) if i in extra else None
-            tbs = [unit_turn(n) for n in group]
-            if i in extra:
-                value_out(extra[i], vacc)
-            for n in group:
-                unit_rope(n, tbs[n - group.start])
-        for b in (2, 3, 4, 5):
-            value_out(b, value_matmul(b))
+        count = {"Q": 0, "T": 0, "P": 0, "V": 0}
+        for letter in "P" + "QQPTTTQ" * 5 + "QQVVTTTQ" + "VT" + "VVV":
+            n = count[letter]
+            if letter == "P":
+                first_pair(n)
+            elif letter == "V":
+                value_out(n, value_matmul(n), 1 if n == 2 * NCHUNK - 1 else 2)
+            elif letter == "Q":
+                unit_matmul(n)
+                if n == 1:
+                    prepare_rest()
+            elif n < count["Q"]:
+                unit_rope(n, unit_turn(n))
+            else:
+                continue
+            count[letter] = n + 1
+        assert count == {"Q": len(units), "T": len(units), "P": TOKENS // P // 2, "V": 2 * NCHUNK}

@@ -46,9 +46,11 @@ def tile_starcoder2attention_pa_kernel(tc, x_words, x_scales, cos, sin, w_words,
             return keep.tile([P, PASSES, width], U8, name=name, align_bytes=64)
 
         xa, wa = code_tile("xa", CHUNK), code_tile("wa", CHUNK)
-        xb, wb, wv = code_tile("xb", 2 * CHUNK), code_tile("wb", MIDDLE), code_tile("wv", KV * D)
+        xb, xc = code_tile("xb", CHUNK), code_tile("xc", CHUNK)
+        wb, wv = code_tile("wb", MIDDLE), code_tile("wv", KV * D)
         xsa, wsa = scale_tile("xsa", CHUNK), scale_tile("wsa", CHUNK)
-        xsb, wsb, wsv = scale_tile("xsb", 2 * CHUNK), scale_tile("wsb", MIDDLE), scale_tile("wsv", KV * D)
+        xsb, xsc = scale_tile("xsb", CHUNK), scale_tile("xsc", CHUNK)
+        wsb, wsv = scale_tile("wsb", MIDDLE), scale_tile("wsv", KV * D)
 
         def load_codes(tile, src, c0, width, g0=0, g1=PASSES):
             nc.sync.dma_start(
@@ -71,6 +73,7 @@ def tile_starcoder2attention_pa_kernel(tc, x_words, x_scales, cos, sin, w_words,
         nc.gpsimd.memset(wsa[:].bitcast(I32), 0)
         nc.vector.memset(wsb[:].bitcast(I32), 0)
         nc.vector.memset(xsb[:].bitcast(I32), 0)
+        nc.vector.memset(xsc[:].bitcast(I32), 0)
         nc.vector.memset(wsv[:].bitcast(I32), 0)
 
         load_codes(xa, x_words, 0, CHUNK, 0, 2)
@@ -79,21 +82,20 @@ def tile_starcoder2attention_pa_kernel(tc, x_words, x_scales, cos, sin, w_words,
         load_scales(wsa, w_scales, 0, CHUNK)
         load_codes(xa, x_words, 0, CHUNK, 2, 4)
         load_codes(wa, w_words, 0, CHUNK, 2, 4)
-        angles = [keep.tile([P, 2, n, HALF], BF16, name="angles%d" % n) for n in (JB, TOKENS // P - JB)]
-        tables = [keep.tile([P, 2, n, D], BF16, name="cs%d" % n) for n in (JB, TOKENS // P - JB)]
+        angles = [keep.tile([P, 2, JB, HALF], BF16, name="angles%d" % c) for c in range(NCHUNK)]
+        tables = [keep.tile([P, 2, JB, D], BF16, name="cs%d" % c) for c in range(NCHUNK)]
 
-        def load_angles(k, t0, t1):
+        def load_angles(c):
             for f, src in ((0, cos), (1, sin)):
-                nc.scalar.dma_start(out=angles[k][:, f, :, :], in_=src[t0:t1, :].rearrange("(b p) i -> p b i", p=P))
+                nc.scalar.dma_start(out=angles[c][:, f, :, :], in_=src[c * CHUNK : (c + 1) * CHUNK, :].rearrange("(b p) i -> p b i", p=P))
 
-        def cs_at(b, n):
-            return tables[0][:, :, b : b + n, :] if b < JB else tables[1][:, :, b - JB : b - JB + n, :]
-
-        load_angles(0, 0, CHUNK)
+        load_angles(0)
         load_codes(wb, w_words, CHUNK, MIDDLE)
         load_scales(wsb, w_scales, CHUNK, MIDDLE)
-        load_codes(xb, x_words, CHUNK, 2 * CHUNK)
-        load_scales(xsb, x_scales, CHUNK, 2 * CHUNK)
+        load_codes(xb, x_words, CHUNK, CHUNK)
+        load_scales(xsb, x_scales, CHUNK, CHUNK)
+        load_codes(xc, x_words, 2 * CHUNK, CHUNK)
+        load_scales(xsc, x_scales, 2 * CHUNK, CHUNK)
         load_codes(wv, w_words, CHUNK + MIDDLE, KV * D)
         load_scales(wsv, w_scales, CHUNK + MIDDLE, KV * D)
 
@@ -137,10 +139,10 @@ def tile_starcoder2attention_pa_kernel(tc, x_words, x_scales, cos, sin, w_words,
         nc.vector.tensor_copy(out=cs[:, 0, :, :].rearrange("p b (a i) -> p b a i", a=2), in_=double(an[:, 0, :, :]))
         nc.vector.tensor_copy(out=cs[:, 1, :, 0:HALF], in_=an[:, 1, :, :])
         nc.vector.tensor_scalar_mul(out=cs[:, 1, :, HALF:D], in0=an[:, 1, :, :], scalar1=-1.0)
-        load_angles(1, CHUNK, TOKENS)
+        load_angles(1)
 
-        def prepare_rest():
-            cs, an = tables[1], angles[1]
+        def prepare(c):
+            cs, an = tables[c], angles[c]
             nc.scalar.copy(out=cs[:, 0, :, :].rearrange("p b (a i) -> p b a i", a=2), in_=double(an[:, 0, :, :]))
             nc.scalar.copy(out=cs[:, 1, :, 0:HALF], in_=an[:, 1, :, :])
             nc.scalar.mul(out=cs[:, 1, :, HALF:D], in_=an[:, 1, :, :], mul=-1.0)
@@ -151,7 +153,8 @@ def tile_starcoder2attention_pa_kernel(tc, x_words, x_scales, cos, sin, w_words,
             return tile[:, g, 2 * a : 2 * (a + width)].bitcast(FP4X4), stile[:, g, a : a + width]
 
         def x_at(g, t0, width):
-            return part((xa, xsa, 0) if t0 < CHUNK else (xb, xsb, CHUNK), g, t0, width)
+            c = t0 // CHUNK
+            return part(((xa, xsa), (xb, xsb), (xc, xsc))[c] + (c * CHUNK,), g, t0, width)
 
         def w_at(g, c0, width):
             for last, pair in ((CHUNK, (wa, wsa, 0)), (CHUNK + MIDDLE, (wb, wsb, CHUNK)), (COLS, (wv, wsv, CHUNK + MIDDLE))):
@@ -174,10 +177,15 @@ def tile_starcoder2attention_pa_kernel(tc, x_words, x_scales, cos, sin, w_words,
 
         def first_pair(b):
             accs = [psum.tile([P, CHUNK], F32, name="facc", tag="kv", bufs=2) for j in range(2)]
-            plane = psum.tile([P, 2, 2, D], F32, name="plane", tag="plane", bufs=1)
             tokens_matmul(accs[0][:], 2 * b * P, 0, CHUNK)
-            for j in range(2):
-                nc.tensor.matmul(plane[:, j, :, :], lhsT=ident_bf[:], rhs=cs_at(2 * b + j, 1)[:, :, 0, :], start=True, stop=True)
+            factors = [tables[2 * b // JB][:, :, (2 * b + j) % JB, :] for j in range(2)]
+            engine = nc.gpsimd
+            if b > 0:
+                engine = nc.vector
+                plane = psum.tile([P, 2, 2, D], F32, name="plane", tag="plane", bufs=1)
+                for j in range(2):
+                    nc.tensor.matmul(plane[:, j, :, :], lhsT=ident_bf[:], rhs=factors[j], start=True, stop=True)
+                    factors[j] = plane[:, j, :, :]
             tokens_matmul(accs[1][:], (2 * b + 1) * P, 0, CHUNK)
             rows = [work.tile([P, FIRST, D], F32, name="rows") for j in range(2)]
             for j in range(2):
@@ -185,10 +193,10 @@ def tile_starcoder2attention_pa_kernel(tc, x_words, x_scales, cos, sin, w_words,
             for j in range(2):
                 t = 2 * b + j
                 m = work.tile([P, 2, CHUNK], F32, name="m", bufs=6)
-                nc.vector.tensor_tensor(
+                engine.tensor_tensor(
                     out=m[:].rearrange("p f (h d) -> p f h d", d=D),
                     in0=rows[j][:].unsqueeze(1).to_broadcast([P, 2, FIRST, D]),
-                    in1=plane[:, j, :, :].unsqueeze(2).to_broadcast([P, 2, FIRST, D]),
+                    in1=factors[j].unsqueeze(2).to_broadcast([P, 2, FIRST, D]),
                     op=MULT,
                 )
                 o = work.tile([P, FIRST, D], F32, name="fo")
@@ -220,45 +228,51 @@ def tile_starcoder2attention_pa_kernel(tc, x_words, x_scales, cos, sin, w_words,
             nc.vector.tensor_tensor(
                 out=m[:],
                 in0=tb[:].unsqueeze(1).to_broadcast([P, 2, CHUNK]),
-                in1=cs_at(c * JB, JB).rearrange("p f j d -> p f (j d)"),
+                in1=tables[c][:].rearrange("p f j d -> p f (j d)"),
                 op=MULT,
             )
             if n % 2 == 0:
                 pairs[n // 2] = work.tile([P, JB, 2, D], F32, name="pair")
             o = pairs[n // 2]
             add_turned(o[:, :, n % 2, :], m)
-            if n % 2 == 1:
-                dst, h0 = (out_q, h - 1) if h < HEADS else (out_k, h - 1 - HEADS)
+            last = n >= len(units) - 2
+            if n % 2 == 1 or last:
+                dst, h1 = (out_q, h + 1) if h < HEADS else (out_k, h + 1 - HEADS)
+                a = n % 2 if last else 0
                 nc.sync.dma_start(
-                    out=dst[0, c * CHUNK : (c + 1) * CHUNK, h0 : h0 + 2, :].rearrange("(j p) h d -> p j h d", p=P), in_=o[:]
+                    out=dst[0, c * CHUNK : (c + 1) * CHUNK, h1 - (n % 2 + 1 - a) : h1, :].rearrange("(j p) h d -> p j h d", p=P),
+                    in_=o[:, :, a : n % 2 + 1, :],
                 )
 
         def value_matmul(b):
-            acc = psum.tile([P, 2, KV * D], F32, name="vacc", tag="kv", bufs=2)
+            acc = psum.tile([P, 2, KV * D], F32, name="vacc", tag="kv" if b < 4 else "q", bufs=2)
             for j in range(2):
                 tokens_matmul(acc[:, j, :], (2 * b + j) * P, (HEADS + KV) * D, KV * D)
             return acc
 
-        def value_out(b, acc, step=2):
+        def value_out(b, acc, queue, step=2):
             for j in range(0, 2, step):
                 y = work.tile([P, step, KV * D], F32, name="vo", bufs=6)
                 nc.vector.tensor_tensor(
                     out=y[:], in0=acc[:, j : j + step, :], in1=value_bias[:].unsqueeze(1).to_broadcast([P, step, KV * D]), op=ADD
                 )
                 t0 = (2 * b + j) * P
-                nc.sync.dma_start(out=out_v[0, t0 : t0 + step * P, :, :].rearrange("(j p) h d -> p j (h d)", p=P), in_=y[:])
+                queue.dma_start(out=out_v[0, t0 : t0 + step * P, :, :].rearrange("(j p) h d -> p j (h d)", p=P), in_=y[:])
 
         count = {"Q": 0, "T": 0, "P": 0, "V": 0}
-        for letter in "P" + "QQPTTTQ" * 5 + "QQVVTTTQ" + "VT" + "VVV":
+        for letter in "PP" + "QQT" + "PQQQTTT" * 4 + "QQVTTT" + "QQVTT" + "VVVV":
             n = count[letter]
             if letter == "P":
                 first_pair(n)
             elif letter == "V":
-                value_out(n, value_matmul(n), 1 if n == 2 * NCHUNK - 1 else 2)
+                value_out(n, value_matmul(n), nc.scalar if n > 2 else nc.sync, 1 if n == 2 * NCHUNK - 1 else 2)
             elif letter == "Q":
                 unit_matmul(n)
-                if n == 1:
-                    prepare_rest()
+                if n == 0:
+                    prepare(1)
+                    load_angles(2)
+                elif n == 4:
+                    prepare(2)
             elif n < count["Q"]:
                 unit_rope(n, unit_turn(n))
             else:

from contextlib import ExitStack

import concourse.mybir as mybir
from concourse.masks import make_identity

F32 = mybir.dt.float32
BF16 = mybir.dt.bfloat16
I32 = mybir.dt.int32
U8 = mybir.dt.uint8
FP4X4 = mybir.dt.float4_e2m1fn_x4
ADD = mybir.AluOpType.add
MULT = mybir.AluOpType.mult
IDENTITY = mybir.ActivationFunctionType.Identity

P = 128
TOKENS = 1536
HIDDEN = 2048
HEADS = 8
KV = 2
D = 128
HALF = 64
COLS = (HEADS + 2 * KV) * D
BLOCKS = COLS // P
PASSES = HIDDEN // 512
CHUNK = 512
NCHUNK = TOKENS // CHUNK
JB = CHUNK // P
MIDDLE = COLS - CHUNK - KV * D
FIRST = 4

FLOPS = 2 * TOKENS * HIDDEN * COLS


def tile_starcoder2attention_pa_kernel(tc, x_words, x_scales, cos, sin, w_words, w_scales, bias, out_q, out_k, out_v):
    nc = tc.nc
    with ExitStack() as ctx:
        ctx.enter_context(tc.manual_schedule())
        keep = ctx.enter_context(tc.tile_pool(name="keep", bufs=1))
        work = ctx.enter_context(tc.tile_pool(name="work", bufs=4))
        psum = ctx.enter_context(tc.psum_pool(name="psum", bufs=2))

        def code_tile(name, width):
            return keep.tile([P, PASSES, 2 * width], U8, name=name, align_bytes=64)

        def scale_tile(name, width):
            return keep.tile([P, PASSES, width], U8, name=name, align_bytes=64)

        xa, wa = code_tile("xa", CHUNK), code_tile("wa", CHUNK)
        xb, xc = code_tile("xb", CHUNK), code_tile("xc", CHUNK)
        wb, wv = code_tile("wb", MIDDLE), code_tile("wv", KV * D)
        xsa, wsa = scale_tile("xsa", CHUNK), scale_tile("wsa", CHUNK)
        xsb, xsc = scale_tile("xsb", CHUNK), scale_tile("xsc", CHUNK)
        wsb, wsv = scale_tile("wsb", MIDDLE), scale_tile("wsv", KV * D)

        def load_codes(tile, src, c0, width, g0=0, g1=PASSES):
            nc.sync.dma_start(
                out=tile[:, g0:g1, :].bitcast(I32),
                in_=src[g0:g1, :, 2 * c0 : 2 * (c0 + width)].rearrange("g p c -> p g c").bitcast(I32),
            )

        def load_scales(tile, src, c0, width):
            for q in range(4):
                nc.sync.dma_start(
                    out=tile[32 * q : 32 * q + 4, :, :].bitcast(I32),
                    in_=src[:, 4 * q : 4 * q + 4, c0 : c0 + width].rearrange("g r n -> r g n").bitcast(I32),
                )

        bias_rows = keep.tile([P, P], BF16, name="bias_rows")
        warm = keep.tile([P, P], BF16, name="warm")
        nc.vector.memset(bias_rows[:], 0.0)
        nc.vector.memset(warm[:], 0.0)
        nc.vector.memset(xsa[:].bitcast(I32), 0)
        nc.gpsimd.memset(wsa[:].bitcast(I32), 0)
        nc.vector.memset(wsb[:].bitcast(I32), 0)
        nc.vector.memset(xsb[:].bitcast(I32), 0)
        nc.vector.memset(xsc[:].bitcast(I32), 0)
        nc.vector.memset(wsv[:].bitcast(I32), 0)

        load_codes(xa, x_words, 0, CHUNK, 0, 2)
        load_codes(wa, w_words, 0, CHUNK, 0, 2)
        load_scales(xsa, x_scales, 0, CHUNK)
        load_scales(wsa, w_scales, 0, CHUNK)
        load_codes(xa, x_words, 0, CHUNK, 2, 4)
        load_codes(wa, w_words, 0, CHUNK, 2, 4)
        angles = [keep.tile([P, 2, JB, HALF], BF16, name="angles%d" % c) for c in range(NCHUNK)]
        tables = [keep.tile([P, 2, JB, D], BF16, name="cs%d" % c) for c in range(NCHUNK)]

        def load_angles(c):
            for f, src in ((0, cos), (1, sin)):
                nc.scalar.dma_start(out=angles[c][:, f, :, :], in_=src[c * CHUNK : (c + 1) * CHUNK, :].rearrange("(b p) i -> p b i", p=P))

        load_angles(0)
        load_codes(wb, w_words, CHUNK, MIDDLE)
        load_scales(wsb, w_scales, CHUNK, MIDDLE)
        load_codes(xb, x_words, CHUNK, CHUNK)
        load_scales(xsb, x_scales, CHUNK, CHUNK)
        load_codes(xc, x_words, 2 * CHUNK, CHUNK)
        load_scales(xsc, x_scales, 2 * CHUNK, CHUNK)
        load_codes(wv, w_words, CHUNK + MIDDLE, KV * D)
        load_scales(wsv, w_scales, CHUNK + MIDDLE, KV * D)

        def double(a):
            return a.unsqueeze(2).to_broadcast([P, a.shape[1], 2, HALF])

        ident_bf = keep.tile([P, P], BF16, name="ident_bf")
        ident = keep.tile([P, P], F32, name="ident")
        nc.gpsimd.dma_start(out=bias_rows[0:BLOCKS, :], in_=bias.rearrange("(a b) -> a b", b=P))
        make_identity(nc, ident_bf[:])

        make_identity(nc, ident[:])

        warm_ps = psum.tile([P, CHUNK], F32, name="warm_ps", tag="t", bufs=3)

        def warm_up(count):
            for unused in range(count):
                nc.tensor.matmul(warm_ps[:], lhsT=warm[:], rhs=warm[:, 0:1].to_broadcast([P, CHUNK]), start=True, stop=True)

        warm_up(7)
        bt_ps = psum.tile([P, P], BF16, name="bt_ps", tag="kv", bufs=2)
        nc.tensor.transpose(bt_ps[:], bias_rows[:], ident_bf[:])
        bias_bf = keep.tile([P, BLOCKS], BF16, name="bias_bf")
        nc.scalar.copy(out=bias_bf[:], in_=bt_ps[:, 0:BLOCKS])
        bias_col = keep.tile([P, BLOCKS], F32, name="bias_col")
        nc.scalar.copy(out=bias_col[:], in_=bt_ps[:, 0:BLOCKS])

        def spread_bias(blocks, name):
            ps = psum.tile([P, CHUNK], F32, name=name + "_ps", tag="q", bufs=2)
            row = keep.tile([P, len(blocks) * P], F32, name=name)
            for i in range(len(blocks)):
                b = blocks[i]
                nc.tensor.matmul(ps[:, i * P : (i + 1) * P], lhsT=bias_bf[:, b : b + 1].to_broadcast([P, P]), rhs=ident_bf[:], start=True, stop=True)
            nc.scalar.copy(out=row[:], in_=ps[:, 0 : len(blocks) * P])
            return row

        value_bias = spread_bias((BLOCKS - 2, BLOCKS - 1), "value_bias")
        first_bias = spread_bias(tuple(range(FIRST)), "first_bias")
        warm_up(3)
        cs, an = tables[0], angles[0]
        nc.vector.tensor_copy(out=cs[:, 0, :, :].rearrange("p b (a i) -> p b a i", a=2), in_=double(an[:, 0, :, :]))
        nc.vector.tensor_copy(out=cs[:, 1, :, 0:HALF], in_=an[:, 1, :, :])
        nc.vector.tensor_scalar_mul(out=cs[:, 1, :, HALF:D], in0=an[:, 1, :, :], scalar1=-1.0)
        load_angles(1)

        def prepare(c):
            cs, an = tables[c], angles[c]
            nc.scalar.copy(out=cs[:, 0, :, :].rearrange("p b (a i) -> p b a i", a=2), in_=double(an[:, 0, :, :]))
            nc.scalar.copy(out=cs[:, 1, :, 0:HALF], in_=an[:, 1, :, :])
            nc.scalar.mul(out=cs[:, 1, :, HALF:D], in_=an[:, 1, :, :], mul=-1.0)

        def part(pair, g, c0, width):
            tile, stile, base = pair
            a = c0 - base
            return tile[:, g, 2 * a : 2 * (a + width)].bitcast(FP4X4), stile[:, g, a : a + width]

        def x_at(g, t0, width):
            c = t0 // CHUNK
            return part(((xa, xsa), (xb, xsb), (xc, xsc))[c] + (c * CHUNK,), g, t0, width)

        def w_at(g, c0, width):
            for last, pair in ((CHUNK, (wa, wsa, 0)), (CHUNK + MIDDLE, (wb, wsb, CHUNK)), (COLS, (wv, wsv, CHUNK + MIDDLE))):
                if c0 < last:
                    return part(pair, g, c0, width)

        def tokens_matmul(out, t0, c0, width):
            for g in range(PASSES):
                xv, xsv = x_at(g, t0, P)
                wv, wsv = w_at(g, c0, width)
                nc.tensor.matmul_mx(out=out, lhsT=xv, lhsT_scale=xsv, rhs=wv, rhs_scale=wsv, start=(g == 0), stop=(g == PASSES - 1))

        def add_turned(out, m):
            nc.gpsimd.tensor_tensor(
                out=out.rearrange("p x (a i) -> p x a i", a=2),
                in0=m[:, 0, :].rearrange("p (x a i) -> p x a i", a=2, i=HALF),
                in1=m[:, 1, :].rearrange("p (x a i) -> p x a i", a=2, i=HALF)[:, :, ::-1, :],
                op=ADD,
            )

        def first_pair(b):
            accs = [psum.tile([P, CHUNK], F32, name="facc", tag="kv", bufs=2) for j in range(2)]
            tokens_matmul(accs[0][:], 2 * b * P, 0, CHUNK)
            factors = [tables[2 * b // JB][:, :, (2 * b + j) % JB, :] for j in range(2)]
            engine = nc.gpsimd
            if b > 0:
                engine = nc.vector
                plane = psum.tile([P, 2, 2, D], F32, name="plane", tag="plane", bufs=1)
                for j in range(2):
                    nc.tensor.matmul(plane[:, j, :, :], lhsT=ident_bf[:], rhs=factors[j], start=True, stop=True)
                    factors[j] = plane[:, j, :, :]
            tokens_matmul(accs[1][:], (2 * b + 1) * P, 0, CHUNK)
            rows = [work.tile([P, FIRST, D], F32, name="rows") for j in range(2)]
            for j in range(2):
                nc.vector.tensor_tensor(out=rows[j][:].rearrange("p h d -> p (h d)"), in0=accs[j][:], in1=first_bias[:], op=ADD)
            for j in range(2):
                t = 2 * b + j
                m = work.tile([P, 2, CHUNK], F32, name="m", bufs=6)
                engine.tensor_tensor(
                    out=m[:].rearrange("p f (h d) -> p f h d", d=D),
                    in0=rows[j][:].unsqueeze(1).to_broadcast([P, 2, FIRST, D]),
                    in1=factors[j].unsqueeze(2).to_broadcast([P, 2, FIRST, D]),
                    op=MULT,
                )
                o = work.tile([P, FIRST, D], F32, name="fo")
                add_turned(o[:], m)
                nc.sync.dma_start(out=out_q[0, t * P : (t + 1) * P, 0:FIRST, :], in_=o[:])

        units = [(c, h) for c in range(NCHUNK) for h in range(FIRST, HEADS + KV)]
        ys, pairs = {}, {}

        def unit_matmul(n):
            c, h = units[n]
            acc = psum.tile([P, CHUNK], F32, name="acc", tag="q", bufs=2)
            for g in range(PASSES):
                wv, wsv = w_at(g, h * D, D)
                xv, xsv = x_at(g, c * CHUNK, CHUNK)
                nc.tensor.matmul_mx(out=acc[:], lhsT=wv, lhsT_scale=wsv, rhs=xv, rhs_scale=xsv, start=(g == 0), stop=(g == PASSES - 1))
            ys[n] = work.tile([P, CHUNK], F32, name="y", bufs=6)
            nc.scalar.activation(out=ys[n][:], in_=acc[:], func=IDENTITY, bias=bias_col[:, h : h + 1])

        def unit_turn(n):
            tb = psum.tile([P, CHUNK], F32, name="tb", tag="t", bufs=3)
            for j in range(JB):
                nc.tensor.transpose(tb[:, j * P : (j + 1) * P], ys[n][:, j * P : (j + 1) * P], ident[:])
            return tb

        def unit_rope(n, tb):
            c, h = units[n]
            m = work.tile([P, 2, CHUNK], F32, name="m", bufs=6)
            nc.vector.tensor_tensor(
                out=m[:],
                in0=tb[:].unsqueeze(1).to_broadcast([P, 2, CHUNK]),
                in1=tables[c][:].rearrange("p f j d -> p f (j d)"),
                op=MULT,
            )
            if n % 2 == 0:
                pairs[n // 2] = work.tile([P, JB, 2, D], F32, name="pair")
            o = pairs[n // 2]
            add_turned(o[:, :, n % 2, :], m)
            last = n >= len(units) - 2
            if n % 2 == 1 or last:
                dst, h1 = (out_q, h + 1) if h < HEADS else (out_k, h + 1 - HEADS)
                a = n % 2 if last else 0
                nc.sync.dma_start(
                    out=dst[0, c * CHUNK : (c + 1) * CHUNK, h1 - (n % 2 + 1 - a) : h1, :].rearrange("(j p) h d -> p j h d", p=P),
                    in_=o[:, :, a : n % 2 + 1, :],
                )

        def value_matmul(b):
            acc = psum.tile([P, 2, KV * D], F32, name="vacc", tag="kv" if b < 4 else "q", bufs=2)
            for j in range(2):
                tokens_matmul(acc[:, j, :], (2 * b + j) * P, (HEADS + KV) * D, KV * D)
            return acc

        def value_out(b, acc, queue, step=2):
            for j in range(0, 2, step):
                y = work.tile([P, step, KV * D], F32, name="vo", bufs=6)
                nc.vector.tensor_tensor(
                    out=y[:], in0=acc[:, j : j + step, :], in1=value_bias[:].unsqueeze(1).to_broadcast([P, step, KV * D]), op=ADD
                )
                t0 = (2 * b + j) * P
                queue.dma_start(out=out_v[0, t0 : t0 + step * P, :, :].rearrange("(j p) h d -> p j (h d)", p=P), in_=y[:])

        count = {"Q": 0, "T": 0, "P": 0, "V": 0}
        for letter in "PP" + "QQT" + "PQQQTTT" * 4 + "QQVTTT" + "QQVTT" + "VVVV":
            n = count[letter]
            if letter == "P":
                first_pair(n)
            elif letter == "V":
                value_out(n, value_matmul(n), nc.scalar if n > 2 else nc.sync, 1 if n == 2 * NCHUNK - 1 else 2)
            elif letter == "Q":
                unit_matmul(n)
                if n == 0:
                    prepare(1)
                    load_angles(2)
                elif n == 4:
                    prepare(2)
            elif n < count["Q"]:
                unit_rope(n, unit_turn(n))
            else:
                continue
            count[letter] = n + 1
        assert count == {"Q": len(units), "T": len(units), "P": TOKENS // P // 2, "V": 2 * NCHUNK}
